import numpy as np
import ml_dtypes


def mxq(x, axis, fmt="e4m3"):
    dtype, down = {"e4m3": (ml_dtypes.float8_e4m3fn, 7), "e5m2": (ml_dtypes.float8_e5m2, 14)}[fmt]
    v = np.moveaxis(np.asarray(x, np.float32).astype(ml_dtypes.bfloat16).astype(np.float64), axis, -1)
    blocks = v.reshape(v.shape[:-1] + (-1, 32))
    amax = np.abs(blocks).max(-1, keepdims=True)
    byte = np.maximum(np.where(amax > 0, np.frexp(amax)[1] - 1 + 127, 0) - down, 1)
    scale = np.exp2(byte - 127.0)
    codes = (blocks / scale).astype(np.float32).astype(dtype).astype(np.float64)
    return np.moveaxis((codes * scale).reshape(v.shape), -1, axis)


WIDE = False


def mx_kscale(k):
    if not WIDE:
        return np.ones(k)
    levels = np.array([10, -10, 5, -5, 0])
    if k % 512:
        return np.exp2(np.random.permutation(np.resize(levels, k // 32))).repeat(32)
    a = np.empty((k // 512, 16))
    for p in range(k // 512):
        a[p, :8] = np.random.permutation(np.resize(levels, 8))
        for g in range(8):
            far = levels[np.abs(levels - a[p, g]) >= 10]
            a[p, g + 8] = far[np.random.randint(len(far))]
    return np.exp2(a.ravel()).repeat(32)


BF16 = ml_dtypes.bfloat16


def bf(x):
    return np.asarray(x, np.float32).astype(BF16)


def f64(x):
    return np.asarray(x).astype(np.float64)


B, Q, K, D = 8, 1024, 512, 512
NEG = -10000.0


def setup_inputs():
    s, t = mx_kscale(D), mx_kscale(D)
    return {"query": bf(np.random.standard_normal((B, Q, D)) * s),
            "context": bf(np.random.standard_normal((B, K, D)) * 0.5 / t),
            "query_bit": bf(np.random.random((B, Q)) > 0.25),
            "context_bit": bf(np.random.random((B, K)) > 0.25),
            "W_in": bf(np.random.standard_normal((D, D)) * 4.0 / D * t[:, None] / s[None, :]),
            "b_in": bf(np.random.standard_normal(D) / np.sqrt(D) * t)}


def reference(query, context, query_bit, context_bit, W_in, b_in):
    ext = (1.0 - f64(query_bit)[:, :, None] * f64(context_bit)[:, None, :]) * NEG
    q = (mxq(f64(query), 2, "e4m3") @ mxq(f64(W_in), 1, "e4m3").T) + f64(b_in)
    scores = (mxq(q, 2, "e4m3") @ mxq(f64(context), 2, "e4m3").transpose(0, 2, 1)) + ext
    e = np.exp(scores - scores.max(-1, keepdims=True))
    return e / e.sum(-1, keepdims=True)

@@ -1,0 +1,231 @@
+from contextlib import ExitStack
+
+import concourse.bass as bass
+import concourse.mybir as mybir
+import concourse.tile as tile
+from concourse.masks import make_identity
+
+F32 = mybir.dt.float32
+BF16 = mybir.dt.bfloat16
+U32 = mybir.dt.uint32
+U8 = mybir.dt.uint8
+FP8X4 = mybir.dt.float8_e4m3fn_x4
+ALU = mybir.AluOpType
+ACT = mybir.ActivationFunctionType
+AX = mybir.AxisListType
+
+P = 128
+B, Q, K, D = 8, 1024, 512, 512
+FLOPS = 2 * (2 * B * Q * D * D)
+UNITS = 2 * B
+
+
+def tile_attention_pa_t_kernel(tc, query, context, query_bit, context_bit, W_in, b_in, out):
+    nc = tc.nc
+    with ExitStack() as ctx:
+        const = ctx.enter_context(tc.tile_pool(name="const", bufs=1))
+        xin = ctx.enter_context(tc.tile_pool(name="xin", bufs=3))
+        work = ctx.enter_context(tc.tile_pool(name="work", bufs=2))
+        soft = ctx.enter_context(tc.tile_pool(name="soft", bufs=4))
+        ps_t = ctx.enter_context(tc.psum_pool(name="ps_t", bufs=2))
+        ps_q = ctx.enter_context(tc.psum_pool(name="ps_q", bufs=3))
+        ps_s = ctx.enter_context(tc.psum_pool(name="ps_s", bufs=3))
+
+        W_sb = const.tile([P, 4, D], BF16, name="W_sb")
+        nc.sync.dma_start(
+            out=W_sb[:],
+            in_=W_in.rearrange("(m t) k -> m t k", t=4),
+        )
+        x_tiles = {}
+        c_tiles = {}
+
+        def load(b):
+            x_sb = xin.tile([P, 8, D], BF16, name="x_sb")
+            nc.sync.dma_start(out=x_sb[:], in_=query[b].rearrange("(p t) k -> p t k", t=8))
+            c_sb = xin.tile([P, 4, D], BF16, name="c_sb")
+            nc.sync.dma_start(out=c_sb[:], in_=context[b].rearrange("(t p) k -> p t k", p=P))
+            x_tiles[b] = x_sb
+            c_tiles[b] = c_sb
+
+        load(0)
+        load(1)
+
+        ident = const.tile([P, P], F32, name="ident")
+        make_identity(nc, ident[:])
+
+        b_bf = const.tile([P, 4], BF16, name="b_bf")
+        qb_bf = const.tile([P, B, 8], BF16, name="qb_bf")
+        with nc.allow_non_contiguous_dma(reason="two small vectors, loaded once"):
+            nc.scalar.dma_start(
+                out=b_bf[:],
+                in_=b_in.rearrange("(m t) -> m t", t=4),
+            )
+            nc.scalar.dma_start(out=qb_bf[:], in_=query_bit.rearrange("b (p t) -> p b t", t=8))
+        cb_all = const.tile([P, B * K], BF16, name="cb_all")
+        nc.scalar.dma_start(out=cb_all[:], in_=context_bit.rearrange("b j -> (b j)").partition_broadcast(P))
+
+        b_f = const.tile([P, 4], F32, name="b_f")
+        nc.vector.tensor_copy(out=b_f[:], in_=b_bf[:])
+        pa = const.tile([P, B * 8], F32, name="pa")
+        nc.vector.tensor_scalar(
+            out=pa[:], in0=qb_bf[:].rearrange("p b t -> p (b t)"), scalar1=10000.0, scalar2=None, op0=ALU.mult
+        )
+        dead = const.tile([P, B * K], BF16, name="dead")
+        nc.vector.tensor_scalar(
+            out=dead[:], in0=cb_all[:], scalar1=-1.0, scalar2=1.0, op0=ALU.mult, op1=ALU.add
+        )
+
+        def transpose_group(src_f32, n_tiles, grouped_f32):
+            for h in range(n_tiles // 2):
+                tp = ps_t.tile([P, 4, P], F32, name="tp")
+                for a in range(2):
+                    for u in range(2):
+                        nc.tensor.transpose(
+                            tp[:, 2 * a + u, :], src_f32[:, 2 * h + a, u : 2 * P : 2], ident[:]
+                        )
+                nc.scalar.copy(
+                    out=grouped_f32[:, 2 * h : 2 * h + 2, :, :],
+                    in_=tp[:].rearrange("p (a u) m -> p a m u", a=2),
+                )
+
+        Wg = const.tile([P, 4, P, 4], BF16, name="Wg", align_bytes=64)
+        Wc = const.tile([P, 4 * P], U32, name="Wc", align_bytes=64)
+        Ws = const.tile([P, 4 * P], U8, name="Ws", align_bytes=64)
+        transpose_group(W_sb[:].bitcast(F32), 4, Wg[:].bitcast(F32))
+        nc.vector.quantize_mx(
+            out=Wc[:].bitcast(FP8X4), scales=Ws[:], in_=Wg[:].rearrange("p t m v -> p (t m v)")
+        )
+
+        ctx_q = {}
+        x_q = {}
+        q_q = {}
+
+        def stage_ctx(b):
+            cg = work.tile([P, 4, P, 4], BF16, name="cg", align_bytes=64)
+            cc = work.tile([P, K], U32, name="cc", align_bytes=64)
+            cs = work.tile([P, K], U8, name="cs", align_bytes=64)
+            transpose_group(c_tiles[b][:].bitcast(F32), 4, cg[:].bitcast(F32))
+            nc.vector.quantize_mx(
+                out=cc[:].bitcast(FP8X4), scales=cs[:], in_=cg[:].rearrange("p t m v -> p (t m v)")
+            )
+            ctx_q[b] = (cc, cs)
+
+        def stage_x(n):
+            b, h = n // 2, n % 2
+            xg = work.tile([P, 4, P, 4], BF16, name="xg", align_bytes=64)
+            xc = work.tile([P, 512], U32, name="xc", align_bytes=64)
+            xs = work.tile([P, 512], U8, name="xs", align_bytes=64)
+            transpose_group(x_tiles[b][:, 4 * h : 4 * h + 4, :].bitcast(F32), 4, xg[:].bitcast(F32))
+            nc.vector.quantize_mx(
+                out=xc[:].bitcast(FP8X4), scales=xs[:], in_=xg[:].rearrange("p t m v -> p (t m v)")
+            )
+            x_q[n] = (xc, xs)
+
+        def stage_q(n):
+            xc, xs = x_q[n]
+            q_bf = work.tile([P, 4, 512], BF16, name="q_bf")
+            for t in range(4):
+                qp = ps_q.tile([P, 512], F32, name="qp")
+                nc.tensor.matmul_mx(
+                    out=qp[:],
+                    lhsT=Wc[:, P * t : P * (t + 1)].bitcast(FP8X4),
+                    lhsT_scale=Ws[:, P * t : P * (t + 1)],
+                    rhs=xc[:].bitcast(FP8X4),
+                    rhs_scale=xs[:],
+                    start=True,
+                    stop=True,
+                )
+                nc.scalar.activation(
+                    out=q_bf[:, t, :], in_=qp[:], func=ACT.Identity, bias=b_f[:, t : t + 1], scale=1.0
+                )
+            qg = work.tile([P, 512, 4], BF16, name="qg", align_bytes=64)
+            qc = work.tile([P, 512], U32, name="qc", align_bytes=64)
+            qs = work.tile([P, 512], U8, name="qs", align_bytes=64)
+            nc.scalar.copy(
+                out=qg[:, 0:192, :].rearrange("p (c i) t -> p c t i", i=4),
+                in_=q_bf[:, :, 0:192].rearrange("p t (c i) -> p c t i", i=4),
+            )
+            nc.vector.tensor_copy(
+                out=qg[:, 192:512, :].rearrange("p (c i) t -> p c t i", i=4),
+                in_=q_bf[:, :, 192:512].rearrange("p t (c i) -> p c t i", i=4),
+            )
+            nc.vector.quantize_mx(
+                out=qc[:].bitcast(FP8X4), scales=qs[:], in_=qg[:].rearrange("p c t -> p (c t)")
+            )
+            q_q[n] = (qc, qs)
+
+        def stage_s(n):
+            b, h = n // 2, n % 2
+            last = n == UNITS - 1
+            qc, qs = q_q[n]
+            cc, cs = ctx_q[b]
+            z = soft.tile([P, 4, K], F32, name="z")
+            nm = soft.tile([P, 4], F32, name="nm")
+            ssum = soft.tile([P, 4], F32, name="ssum")
+            r = soft.tile([P, 4], F32, name="r")
+            for k in range(4):
+                sp = ps_s.tile([P, K], F32, name="sp")
+                nc.tensor.matmul_mx(
+                    out=sp[:],
+                    lhsT=qc[:, P * k : P * (k + 1)].bitcast(FP8X4),
+                    lhsT_scale=qs[:, P * k : P * (k + 1)],
+                    rhs=cc[:].bitcast(FP8X4),
+                    rhs_scale=cs[:],
+                    start=True,
+                    stop=True,
+                )
+                col = 8 * b + 4 * h + k
+                nc.vector.scalar_tensor_tensor(
+                    out=z[:, k, :],
+                    in0=dead[:, K * b : K * (b + 1)],
+                    scalar=pa[:, col : col + 1],
+                    in1=sp[:],
+                    op0=ALU.mult,
+                    op1=ALU.subtract,
+                )
+                if last:
+                    nc.vector.tensor_reduce(out=nm[:, k : k + 1], in_=z[:, k, :], axis=AX.X, op=ALU.min)
+            if not last:
+                nc.vector.tensor_reduce(out=nm[:], in_=z[:], axis=AX.X, op=ALU.min)
+            for k in range(4):
+                nc.scalar.activation(
+                    out=z[:, k, :],
+                    in_=z[:, k, :],
+                    func=ACT.Exp,
+                    bias=nm[:, k : k + 1],
+                    scale=-1.0,
+                    accum_out=ssum[:, k : k + 1],
+                )
+            rows = out[b].rearrange("(p t) j -> p t j", t=8)
+            if last:
+                for k in range(4):
+                    nc.vector.reciprocal(out=r[:, k : k + 1], in_=ssum[:, k : k + 1])
+                    nc.vector.tensor_scalar(
+                        out=z[:, k, :], in0=z[:, k, :], scalar1=r[:, k : k + 1], scalar2=None, op0=ALU.mult
+                    )
+                    nc.sync.dma_start(out=rows[:, 4 * h + k, :], in_=z[:, k, :])
+            else:
+                nc.vector.reciprocal(out=r[:], in_=ssum[:])
+                for k in range(4):
+                    nc.gpsimd.tensor_scalar(
+                        out=z[:, k, :],
+                        in0=z[:, k, :],
+                        scalar1=r[:, k : k + 1],
+                        scalar2=0.0,
+                        op0=ALU.mult,
+                        op1=ALU.add,
+                    )
+                nc.sync.dma_start(out=rows[:, 4 * h : 4 * h + 4, :], in_=z[:])
+
+        for n in range(UNITS + 2):
+            if n < UNITS:
+                b, h = n // 2, n % 2
+                if h == 0:
+                    if b + 2 < B:
+                        load(b + 2)
+                    stage_ctx(b)
+                stage_x(n)
+            if 1 <= n <= UNITS:
+                stage_q(n - 1)
+            if n >= 2:
+                stage_s(n - 2)

@@ -18,214 +18,401 @@ P = 128
 B, Q, K, D = 8, 1024, 512, 512
 FLOPS = 2 * (2 * B * Q * D * D)
 UNITS = 2 * B
+S_COL = 384
+AHEAD = 6
 
 
 def tile_attention_pa_t_kernel(tc, query, context, query_bit, context_bit, W_in, b_in, out):
     nc = tc.nc
     with ExitStack() as ctx:
         const = ctx.enter_context(tc.tile_pool(name="const", bufs=1))
-        xin = ctx.enter_context(tc.tile_pool(name="xin", bufs=3))
-        work = ctx.enter_context(tc.tile_pool(name="work", bufs=2))
+        xin = ctx.enter_context(tc.tile_pool(name="xin", bufs=AHEAD + 1))
+        cin = ctx.enter_context(tc.tile_pool(name="cin", bufs=4))
+        work = ctx.enter_context(tc.tile_pool(name="work", bufs=3))
+        keep = ctx.enter_context(tc.tile_pool(name="keep", bufs=4))
         soft = ctx.enter_context(tc.tile_pool(name="soft", bufs=4))
-        ps_t = ctx.enter_context(tc.psum_pool(name="ps_t", bufs=2))
-        ps_q = ctx.enter_context(tc.psum_pool(name="ps_q", bufs=3))
+        ps_t = ctx.enter_context(tc.psum_pool(name="ps_t", bufs=3))
+        ps_q = ctx.enter_context(tc.psum_pool(name="ps_q", bufs=2))
         ps_s = ctx.enter_context(tc.psum_pool(name="ps_s", bufs=3))
-
-        W_sb = const.tile([P, 4, D], BF16, name="W_sb")
-        nc.sync.dma_start(
-            out=W_sb[:],
-            in_=W_in.rearrange("(m t) k -> m t k", t=4),
-        )
-        x_tiles = {}
-        c_tiles = {}
-
-        def load(b):
-            x_sb = xin.tile([P, 8, D], BF16, name="x_sb")
-            nc.sync.dma_start(out=x_sb[:], in_=query[b].rearrange("(p t) k -> p t k", t=8))
-            c_sb = xin.tile([P, 4, D], BF16, name="c_sb")
-            nc.sync.dma_start(out=c_sb[:], in_=context[b].rearrange("(t p) k -> p t k", p=P))
-            x_tiles[b] = x_sb
-            c_tiles[b] = c_sb
-
-        load(0)
-        load(1)
-
         ident = const.tile([P, P], F32, name="ident")
         make_identity(nc, ident[:])
+        ctx.enter_context(tc.manual_schedule())
 
+        x_raw, c_raw, cb_raw = {}, {}, {}
+        banks = {}
+        xg, xq, qb16, qg, qq = {}, {}, {}, {}, {}
+        cg, cq = {}, {}
+        dead = {}
+        zs, sums, mins, recs = {}, {}, {}, {}
+
+        def load_x(n):
+            b, h = n // 2, n % 2
+            x_sb = xin.tile([P, 4, D], BF16, name="x_sb")
+            nc.sync.dma_start(
+                out=x_sb[:], in_=query[b].rearrange("(p t) k -> p t k", t=8)[:, 4 * h : 4 * h + 4, :]
+            )
+            x_raw[n] = x_sb
+
+        def load_c(b):
+            c_sb = cin.tile([P, 4, D], BF16, name="c_sb")
+            nc.sync.dma_start(out=c_sb[:], in_=context[b].rearrange("(t p) k -> p t k", p=P))
+            c_raw[b] = c_sb
+
+        def load_cb(b):
+            cb = cin.tile([P, K], BF16, name="cb")
+            nc.sync.dma_start(out=cb[:], in_=context_bit[b].partition_broadcast(P))
+            cb_raw[b] = cb
+
+        def load(n):
+            if n >= UNITS:
+                return
+            load_x(n)
+            if n % 2 == 0:
+                load_c(n // 2)
+                load_cb(n // 2)
+
+        W_sb = const.tile([P, 4, D], BF16, name="W_sb")
+        nc.sync.dma_start(out=W_sb[:], in_=W_in.rearrange("(m t) k -> m t k", t=4))
         b_bf = const.tile([P, 4], BF16, name="b_bf")
         qb_bf = const.tile([P, B, 8], BF16, name="qb_bf")
         with nc.allow_non_contiguous_dma(reason="two small vectors, loaded once"):
-            nc.scalar.dma_start(
-                out=b_bf[:],
-                in_=b_in.rearrange("(m t) -> m t", t=4),
-            )
+            nc.scalar.dma_start(out=b_bf[:], in_=b_in.rearrange("(m t) -> m t", t=4))
             nc.scalar.dma_start(out=qb_bf[:], in_=query_bit.rearrange("b (p t) -> p b t", t=8))
-        cb_all = const.tile([P, B * K], BF16, name="cb_all")
-        nc.scalar.dma_start(out=cb_all[:], in_=context_bit.rearrange("b j -> (b j)").partition_broadcast(P))
+        for n in range(AHEAD):
+            load(n)
 
-        b_f = const.tile([P, 4], F32, name="b_f")
-        nc.vector.tensor_copy(out=b_f[:], in_=b_bf[:])
-        pa = const.tile([P, B * 8], F32, name="pa")
-        nc.vector.tensor_scalar(
-            out=pa[:], in0=qb_bf[:].rearrange("p b t -> p (b t)"), scalar1=10000.0, scalar2=None, op0=ALU.mult
-        )
-        dead = const.tile([P, B * K], BF16, name="dead")
-        nc.vector.tensor_scalar(
-            out=dead[:], in0=cb_all[:], scalar1=-1.0, scalar2=1.0, op0=ALU.mult, op1=ALU.add
-        )
+        warm = const.tile([P, 1], F32, name="warm")
+        nc.vector.memset(warm[:], 0.0)
+        nc.scalar.activation(out=warm[:], in_=warm[:], func=ACT.Exp)
 
-        def transpose_group(src_f32, n_tiles, grouped_f32):
-            for h in range(n_tiles // 2):
-                tp = ps_t.tile([P, 4, P], F32, name="tp")
-                for a in range(2):
-                    for u in range(2):
-                        nc.tensor.transpose(
-                            tp[:, 2 * a + u, :], src_f32[:, 2 * h + a, u : 2 * P : 2], ident[:]
-                        )
-                nc.scalar.copy(
-                    out=grouped_f32[:, 2 * h : 2 * h + 2, :, :],
-                    in_=tp[:].rearrange("p (a u) m -> p a m u", a=2),
+        zeros = const.tile([P, 512], BF16, name="zeros")
+        nc.vector.memset(zeros[:], 0.0)
+
+        def idle_matmuls(count):
+            idle = ps_s.tile([P, 512], F32, name="sp")
+            for j in range(count):
+                nc.tensor.matmul(idle[:], lhsT=zeros[:, 0:P], rhs=zeros[:], start=True, stop=True)
+
+        def transposes(src, row, key):
+            tp = ps_t.tile([P, 4, P], F32, name="tp")
+            for a in range(2):
+                for u in range(2):
+                    nc.tensor.transpose(tp[:, 2 * a + u, :], src[:, row + a, u : 2 * P : 2], ident[:])
+            banks[key] = tp
+
+        def bank_copy(copy, dst, key):
+            tp = banks[key]
+            copy(out=dst, in_=tp[:].rearrange("p (a u) m -> p a m u", a=2))
+
+        def t_x(n, pair):
+            transposes(x_raw[n][:].bitcast(F32), 2 * pair, ("x", n, pair))
+
+        def c_x(n, pair, copy):
+            if n not in xg:
+                g = work.tile([P, 4, P, 4], BF16, name="g", align_bytes=64)
+                xg[n] = g
+            bank_copy(copy, xg[n][:].bitcast(F32)[:, 2 * pair : 2 * pair + 2, :, :], ("x", n, pair))
+
+        def q_x(n):
+            xc = keep.tile([P, 512], U32, name="xc", align_bytes=64)
+            xs = keep.tile([P, 512], U8, name="xs", align_bytes=64)
+            nc.vector.quantize_mx(
+                out=xc[:].bitcast(FP8X4), scales=xs[:], in_=xg[n][:].rearrange("p t m v -> p (t m v)")
+            )
+            xq[n] = (xc, xs)
+
+        def t_c(i):
+            transposes(c_raw[i // 2][:].bitcast(F32), 2 * (i % 2), ("c", i))
+
+        def c_c(i, copy):
+            g = work.tile([P, 2, P, 4], BF16, name="cgrp", align_bytes=64)
+            cg[i] = g
+            bank_copy(copy, g[:].bitcast(F32), ("c", i))
+
+        def q_c(i):
+            b, half = i // 2, i % 2
+            if half == 0:
+                cc = keep.tile([P, K], U32, name="cc", align_bytes=64)
+                cs = keep.tile([P, K], U8, name="cs", align_bytes=64)
+                cq[b] = (cc, cs)
+            cc, cs = cq[b]
+            cols = slice(256 * half, 256 * half + 256)
+            nc.vector.quantize_mx(
+                out=cc[:, cols].bitcast(FP8X4),
+                scales=cs[:, cols],
+                in_=cg[i][:].rearrange("p t m v -> p (t m v)"),
+            )
+
+        def m1(n, t, in_score_bank=False):
+            xc, xs = xq[n]
+            if in_score_bank:
+                qp = ps_s.tile([P, 512], F32, name="sp")
+            else:
+                qp = ps_q.tile([P, 512], F32, name="qp")
+            nc.tensor.matmul_mx(
+                out=qp[:],
+                lhsT=Wc[:, P * t : P * (t + 1)].bitcast(FP8X4),
+                lhsT_scale=Ws[:, P * t : P * (t + 1)],
+                rhs=xc[:].bitcast(FP8X4),
+                rhs_scale=xs[:],
+                start=True,
+                stop=True,
+            )
+            banks["q", n, t] = qp
+
+        def drain(n, t, on_vector=False):
+            if n not in qb16:
+                q_bf = work.tile([P, 4, 512], BF16, name="q_bf")
+                qb16[n] = q_bf
+            qp = banks["q", n, t]
+            if on_vector:
+                nc.vector.tensor_scalar(
+                    out=qb16[n][:, t, :], in0=qp[:], scalar1=b_f[:, t : t + 1], scalar2=None, op0=ALU.add
+                )
+            else:
+                nc.scalar.activation(
+                    out=qb16[n][:, t, :], in_=qp[:], func=ACT.Identity, bias=b_f[:, t : t + 1], scale=1.0
                 )
 
+        def regroup(n, lo, hi, copy):
+            if n not in qg:
+                g = work.tile([P, 512, 4], BF16, name="qg", align_bytes=64)
+                qg[n] = g
+            copy(
+                out=qg[n][:, lo:hi, :].rearrange("p (c i) t -> p c t i", i=4),
+                in_=qb16[n][:, :, lo:hi].rearrange("p t (c i) -> p c t i", i=4),
+            )
+
+        def q_q(n, half):
+            if half == 0:
+                qc = keep.tile([P, 512], U32, name="qc", align_bytes=64)
+                qs = keep.tile([P, 512], U8, name="qs", align_bytes=64)
+                qq[n] = (qc, qs)
+            qc, qs = qq[n]
+            cols = slice(256 * half, 256 * half + 256)
+            nc.vector.quantize_mx(
+                out=qc[:, cols].bitcast(FP8X4),
+                scales=qs[:, cols],
+                in_=qg[n][:, cols, :].rearrange("p c t -> p (c t)"),
+            )
+
+        def m2(n, k):
+            qc, qs = qq[n]
+            cc, cs = cq[n // 2]
+            sp = ps_s.tile([P, K], F32, name="sp")
+            nc.tensor.matmul_mx(
+                out=sp[:],
+                lhsT=qc[:, P * k : P * (k + 1)].bitcast(FP8X4),
+                lhsT_scale=qs[:, P * k : P * (k + 1)],
+                rhs=cc[:].bitcast(FP8X4),
+                rhs_scale=cs[:],
+                start=True,
+                stop=True,
+            )
+            banks["s", n, k] = sp
+
+        def make_dead(b):
+            d = keep.tile([P, K], BF16, name="dead")
+            nc.vector.tensor_scalar(
+                out=d[:], in0=cb_raw[b][:], scalar1=-1.0, scalar2=1.0, op0=ALU.mult, op1=ALU.add
+            )
+            dead[b] = d
+
+        def mask(n, k):
+            if k == 0:
+                z = soft.tile([P, 4, K], F32, name="z")
+                nm = soft.tile([P, 4], F32, name="nm")
+                ssum = soft.tile([P, 4], F32, name="ssum")
+                r = soft.tile([P, 4], F32, name="r")
+                zs[n], mins[n], sums[n], recs[n] = z, nm, ssum, r
+            col = 4 * n + k
+            nc.vector.scalar_tensor_tensor(
+                out=zs[n][:, k, :],
+                in0=dead[n // 2][:],
+                scalar=pa[:, col : col + 1],
+                in1=banks["s", n, k][:],
+                op0=ALU.mult,
+                op1=ALU.subtract,
+            )
+
+        def row_min(n, lo, hi):
+            nc.vector.tensor_reduce(out=mins[n][:, lo:hi], in_=zs[n][:, lo:hi, :], axis=AX.X, op=ALU.min)
+
+        def exp(n, k):
+            nc.scalar.activation(
+                out=zs[n][:, k, :],
+                in_=zs[n][:, k, :],
+                func=ACT.Exp,
+                bias=mins[n][:, k : k + 1],
+                scale=-1.0,
+                accum_out=sums[n][:, k : k + 1],
+            )
+
+        def recip(n, lo, hi):
+            nc.vector.reciprocal(out=recs[n][:, lo:hi], in_=sums[n][:, lo:hi])
+
+        def norm_g(n, k):
+            nc.gpsimd.tensor_scalar(
+                out=zs[n][:, k, :],
+                in0=zs[n][:, k, :],
+                scalar1=recs[n][:, k : k + 1],
+                scalar2=0.0,
+                op0=ALU.mult,
+                op1=ALU.add,
+            )
+
+        def norm_v(n, k):
+            nc.vector.tensor_scalar(
+                out=zs[n][:, k, :], in0=zs[n][:, k, :], scalar1=recs[n][:, k : k + 1], scalar2=None, op0=ALU.mult
+            )
+
+        def store(n, lo, hi):
+            b, h = n // 2, n % 2
+            rows = out[b].rearrange("(p t) j -> p t j", t=8)
+            nc.sync.dma_start(out=rows[:, 4 * h + lo : 4 * h + hi, :], in_=zs[n][:, lo:hi, :])
+
+        vcopy = nc.vector.tensor_copy
+        scopy = nc.scalar.copy
+
+        b_f = const.tile([P, 4], F32, name="b_f")
+        pa = const.tile([P, B * 8], F32, name="pa")
         Wg = const.tile([P, 4, P, 4], BF16, name="Wg", align_bytes=64)
         Wc = const.tile([P, 4 * P], U32, name="Wc", align_bytes=64)
         Ws = const.tile([P, 4 * P], U8, name="Ws", align_bytes=64)
-        transpose_group(W_sb[:].bitcast(F32), 4, Wg[:].bitcast(F32))
+        idle_matmuls(7)
+        transposes(W_sb[:].bitcast(F32), 0, ("w", 0))
+        transposes(W_sb[:].bitcast(F32), 2, ("w", 1))
+        bank_copy(scopy, Wg[:].bitcast(F32)[:, 0:2, :, :], ("w", 0))
+        bank_copy(vcopy, Wg[:].bitcast(F32)[:, 2:4, :, :], ("w", 1))
+        t_x(0, 0)
+        idle_matmuls(2)
+        t_x(0, 1)
         nc.vector.quantize_mx(
             out=Wc[:].bitcast(FP8X4), scales=Ws[:], in_=Wg[:].rearrange("p t m v -> p (t m v)")
         )
-
-        ctx_q = {}
-        x_q = {}
-        q_q = {}
-
-        def stage_ctx(b):
-            cg = work.tile([P, 4, P, 4], BF16, name="cg", align_bytes=64)
-            cc = work.tile([P, K], U32, name="cc", align_bytes=64)
-            cs = work.tile([P, K], U8, name="cs", align_bytes=64)
-            transpose_group(c_tiles[b][:].bitcast(F32), 4, cg[:].bitcast(F32))
-            nc.vector.quantize_mx(
-                out=cc[:].bitcast(FP8X4), scales=cs[:], in_=cg[:].rearrange("p t m v -> p (t m v)")
-            )
-            ctx_q[b] = (cc, cs)
-
-        def stage_x(n):
-            b, h = n // 2, n % 2
-            xg = work.tile([P, 4, P, 4], BF16, name="xg", align_bytes=64)
-            xc = work.tile([P, 512], U32, name="xc", align_bytes=64)
-            xs = work.tile([P, 512], U8, name="xs", align_bytes=64)
-            transpose_group(x_tiles[b][:, 4 * h : 4 * h + 4, :].bitcast(F32), 4, xg[:].bitcast(F32))
-            nc.vector.quantize_mx(
-                out=xc[:].bitcast(FP8X4), scales=xs[:], in_=xg[:].rearrange("p t m v -> p (t m v)")
-            )
-            x_q[n] = (xc, xs)
-
-        def stage_q(n):
-            xc, xs = x_q[n]
-            q_bf = work.tile([P, 4, 512], BF16, name="q_bf")
-            for t in range(4):
-                qp = ps_q.tile([P, 512], F32, name="qp")
-                nc.tensor.matmul_mx(
-                    out=qp[:],
-                    lhsT=Wc[:, P * t : P * (t + 1)].bitcast(FP8X4),
-                    lhsT_scale=Ws[:, P * t : P * (t + 1)],
-                    rhs=xc[:].bitcast(FP8X4),
-                    rhs_scale=xs[:],
-                    start=True,
-                    stop=True,
-                )
-                nc.scalar.activation(
-                    out=q_bf[:, t, :], in_=qp[:], func=ACT.Identity, bias=b_f[:, t : t + 1], scale=1.0
-                )
-            qg = work.tile([P, 512, 4], BF16, name="qg", align_bytes=64)
-            qc = work.tile([P, 512], U32, name="qc", align_bytes=64)
-            qs = work.tile([P, 512], U8, name="qs", align_bytes=64)
-            nc.scalar.copy(
-                out=qg[:, 0:192, :].rearrange("p (c i) t -> p c t i", i=4),
-                in_=q_bf[:, :, 0:192].rearrange("p t (c i) -> p c t i", i=4),
-            )
-            nc.vector.tensor_copy(
-                out=qg[:, 192:512, :].rearrange("p (c i) t -> p c t i", i=4),
-                in_=q_bf[:, :, 192:512].rearrange("p t (c i) -> p c t i", i=4),
-            )
-            nc.vector.quantize_mx(
-                out=qc[:].bitcast(FP8X4), scales=qs[:], in_=qg[:].rearrange("p c t -> p (c t)")
-            )
-            q_q[n] = (qc, qs)
-
-        def stage_s(n):
-            b, h = n // 2, n % 2
-            last = n == UNITS - 1
-            qc, qs = q_q[n]
-            cc, cs = ctx_q[b]
-            z = soft.tile([P, 4, K], F32, name="z")
-            nm = soft.tile([P, 4], F32, name="nm")
-            ssum = soft.tile([P, 4], F32, name="ssum")
-            r = soft.tile([P, 4], F32, name="r")
-            for k in range(4):
-                sp = ps_s.tile([P, K], F32, name="sp")
-                nc.tensor.matmul_mx(
-                    out=sp[:],
-                    lhsT=qc[:, P * k : P * (k + 1)].bitcast(FP8X4),
-                    lhsT_scale=qs[:, P * k : P * (k + 1)],
-                    rhs=cc[:].bitcast(FP8X4),
-                    rhs_scale=cs[:],
-                    start=True,
-                    stop=True,
-                )
-                col = 8 * b + 4 * h + k
-                nc.vector.scalar_tensor_tensor(
-                    out=z[:, k, :],
-                    in0=dead[:, K * b : K * (b + 1)],
-                    scalar=pa[:, col : col + 1],
-                    in1=sp[:],
-                    op0=ALU.mult,
-                    op1=ALU.subtract,
-                )
-                if last:
-                    nc.vector.tensor_reduce(out=nm[:, k : k + 1], in_=z[:, k, :], axis=AX.X, op=ALU.min)
+        c_x(0, 0, scopy)
+        c_x(0, 1, scopy)
+        t_c(0)
+        t_c(1)
+        nc.vector.tensor_copy(out=b_f[:], in_=b_bf[:])
+        q_x(0)
+        c_c(0, vcopy)
+        c_c(1, scopy)
+        idle_matmuls(2)
+        for t in range(4):
+            m1(0, t, in_score_bank=(t >= 2))
+        drain(0, 0)
+        q_c(0)
+        drain(0, 1, on_vector=True)
+        q_c(1)
+        drain(0, 2)
+        drain(0, 3, on_vector=True)
+        t_x(1, 0)
+        t_x(1, 1)
+        c_x(1, 0, scopy)
+        make_dead(0)
+        regroup(0, 0, 256, vcopy)
+        regroup(0, 320, 512, scopy)
+        regroup(0, 256, 320, vcopy)
+        q_q(0, 0)
+        nc.vector.tensor_scalar(
+            out=pa[:], in0=qb_bf[:].rearrange("p b t -> p (b t)"), scalar1=10000.0, scalar2=None, op0=ALU.mult
+        )
+        c_x(1, 1, scopy)
+        q_q(0, 1)
+        t_x(2, 0)
+        t_x(2, 1)
+        for k in range(3):
+            m2(0, k)
+        q_x(1)
+        c_x(2, 0, scopy)
+        c_x(2, 1, scopy)
+        m1(1, 0)
+        m1(1, 1)
+        m2(0, 3)
+        for t in range(4):
+            drain(1, t)
+            if t < 2:
+                m1(1, t + 2)
+        regroup(1, S_COL, 512, scopy)
+        t_x(3, 0)
+        t_c(2)
+        idle_matmuls(2)
+        t_x(3, 1)
+        for i in range(UNITS):
+            last = i == UNITS - 1
+            mask(i, 0)
+            if i > 0:
+                m2(i, 2)
+                m2(i, 3)
+                exp(i - 1, 2)
+                exp(i - 1, 3)
+            mask(i, 1)
+            mask(i, 2)
+            if i == 0:
+                q_x(2)
+            if i > 0:
+                recip(i - 1, 0, 4)
+                for k in range(4):
+                    norm_g(i - 1, k)
+                store(i - 1, 0, 4)
+            load(i + AHEAD)
             if not last:
-                nc.vector.tensor_reduce(out=nm[:], in_=z[:], axis=AX.X, op=ALU.min)
-            for k in range(4):
-                nc.scalar.activation(
-                    out=z[:, k, :],
-                    in_=z[:, k, :],
-                    func=ACT.Exp,
-                    bias=nm[:, k : k + 1],
-                    scale=-1.0,
-                    accum_out=ssum[:, k : k + 1],
-                )
-            rows = out[b].rearrange("(p t) j -> p t j", t=8)
-            if last:
-                for k in range(4):
-                    nc.vector.reciprocal(out=r[:, k : k + 1], in_=ssum[:, k : k + 1])
-                    nc.vector.tensor_scalar(
-                        out=z[:, k, :], in0=z[:, k, :], scalar1=r[:, k : k + 1], scalar2=None, op0=ALU.mult
-                    )
-                    nc.sync.dma_start(out=rows[:, 4 * h + k, :], in_=z[:, k, :])
+                mask(i, 3)
+                row_min(i, 0, 2)
+                row_min(i, 2, 4)
+            if i + 3 < UNITS:
+                c_x(i + 3, 0, scopy)
+            if i + 2 < UNITS:
+                m1(i + 2, 0)
+                drain(i + 2, 0)
+            if i + 3 < UNITS:
+                c_x(i + 3, 1, scopy)
+            if i + 2 < UNITS:
+                c_c(i + 2, scopy if i > 0 else vcopy)
+            if i + 4 < UNITS:
+                t_x(i + 4, 0)
+            if i + 2 < UNITS:
+                m1(i + 2, 1)
+                drain(i + 2, 1)
+            if i + 4 < UNITS:
+                t_x(i + 4, 1)
+            if i + 2 < UNITS:
+                m1(i + 2, 2)
+            if i + 3 < UNITS:
+                t_c(i + 3)
+            if not last:
+                exp(i, 0)
+                exp(i, 1)
+                if i + 2 < UNITS:
+                    m1(i + 2, 3)
+                    drain(i + 2, 2)
+                    drain(i + 2, 3)
+                    regroup(i + 2, S_COL, 512, scopy)
+                    q_c(i + 2)
+                regroup(i + 1, 0, 256, vcopy)
+                regroup(i + 1, 256, S_COL, vcopy)
+                if i % 2 == 1:
+                    make_dead((i + 1) // 2)
+                q_q(i + 1, 0)
+                if i + 3 < UNITS:
+                    q_x(i + 3)
+                q_q(i + 1, 1)
+                m2(i + 1, 0)
+                m2(i + 1, 1)
             else:
-                nc.vector.reciprocal(out=r[:], in_=ssum[:])
+                row_min(i, 0, 1)
+                row_min(i, 1, 2)
+                mask(i, 3)
+                row_min(i, 2, 3)
+                row_min(i, 3, 4)
                 for k in range(4):
-                    nc.gpsimd.tensor_scalar(
-                        out=z[:, k, :],
-                        in0=z[:, k, :],
-                        scalar1=r[:, k : k + 1],
-                        scalar2=0.0,
-                        op0=ALU.mult,
-                        op1=ALU.add,
-                    )
-                nc.sync.dma_start(out=rows[:, 4 * h : 4 * h + 4, :], in_=z[:])
-
-        for n in range(UNITS + 2):
-            if n < UNITS:
-                b, h = n // 2, n % 2
-                if h == 0:
-                    if b + 2 < B:
-                        load(b + 2)
-                    stage_ctx(b)
-                stage_x(n)
-            if 1 <= n <= UNITS:
-                stage_q(n - 1)
-            if n >= 2:
-                stage_s(n - 2)
+                    exp(i, k)
+                recip(i, 0, 2)
+                norm_v(i, 0)
+                norm_v(i, 1)
+                store(i, 0, 2)
+                for k in range(2, 4):
+                    recip(i, k, k + 1)
+                    norm_v(i, k)
+                    store(i, k, k + 1)

@@ -19,6 +19,7 @@ B, Q, K, D = 8, 1024, 512, 512
 FLOPS = 2 * (2 * B * Q * D * D)
 UNITS = 2 * B
 S_COL = 384
+IDLE = 1
 AHEAD = 6
 
 
@@ -345,48 +346,47 @@ def tile_attention_pa_t_kernel(tc, query, context, query_bit, context_bit, W_in,
             if i > 0:
                 m2(i, 2)
                 m2(i, 3)
-                exp(i - 1, 2)
-                exp(i - 1, 3)
-            mask(i, 1)
-            mask(i, 2)
-            if i == 0:
-                q_x(2)
-            if i > 0:
                 recip(i - 1, 0, 4)
                 for k in range(4):
                     norm_g(i - 1, k)
                 store(i - 1, 0, 4)
             load(i + AHEAD)
+            mask(i, 1)
+            if i == 0:
+                q_x(2)
             if not last:
+                mask(i, 2)
                 mask(i, 3)
                 row_min(i, 0, 2)
                 row_min(i, 2, 4)
             if i + 3 < UNITS:
                 c_x(i + 3, 0, scopy)
             if i + 2 < UNITS:
-                m1(i + 2, 0)
+                if i == 0:
+                    m1(i + 2, 0)
                 drain(i + 2, 0)
             if i + 3 < UNITS:
                 c_x(i + 3, 1, scopy)
             if i + 2 < UNITS:
+                m1(i + 2, 1)
                 c_c(i + 2, scopy if i > 0 else vcopy)
             if i + 4 < UNITS:
                 t_x(i + 4, 0)
             if i + 2 < UNITS:
-                m1(i + 2, 1)
                 drain(i + 2, 1)
+                m1(i + 2, 2)
+                drain(i + 2, 2)
             if i + 4 < UNITS:
                 t_x(i + 4, 1)
             if i + 2 < UNITS:
-                m1(i + 2, 2)
+                m1(i + 2, 3)
             if i + 3 < UNITS:
+                idle_matmuls(IDLE)
                 t_c(i + 3)
             if not last:
-                exp(i, 0)
-                exp(i, 1)
+                for k in range(4):
+                    exp(i, k)
                 if i + 2 < UNITS:
-                    m1(i + 2, 3)
-                    drain(i + 2, 2)
                     drain(i + 2, 3)
                     regroup(i + 2, S_COL, 512, scopy)
                     q_c(i + 2)
@@ -400,8 +400,11 @@ def tile_attention_pa_t_kernel(tc, query, context, query_bit, context_bit, W_in,
                 q_q(i + 1, 1)
                 m2(i + 1, 0)
                 m2(i + 1, 1)
+                if i + 3 < UNITS:
+                    m1(i + 3, 0)
             else:
                 row_min(i, 0, 1)
+                mask(i, 2)
                 row_min(i, 1, 2)
                 mask(i, 3)
                 row_min(i, 2, 3)

@@ -18,8 +18,10 @@ P = 128
 B, Q, K, D = 8, 1024, 512, 512
 FLOPS = 2 * (2 * B * Q * D * D)
 UNITS = 2 * B
-S_COL = 384
+S_COL = 320
 IDLE = 1
+G_COL = 384
+T_COL, Z_COL = 192, 128
 AHEAD = 6
 
 
@@ -184,6 +186,26 @@ def tile_attention_pa_t_kernel(tc, query, context, query_bit, context_bit, W_in,
                 in_=qb16[n][:, :, lo:hi].rearrange("p t (c i) -> p c t i", i=4),
             )
 
+        def regroup_g(n, lo, hi):
+            nc.gpsimd.tensor_scalar(
+                out=qg[n][:, lo:hi, :].rearrange("p (c i) t -> p c t i", i=4),
+                in0=qb16[n][:, :, lo:hi].rearrange("p t (c i) -> p c t i", i=4),
+                scalar1=1.0,
+                scalar2=0.0,
+                op0=ALU.mult,
+                op1=ALU.add,
+            )
+
+        def s_col(n):
+            if n == UNITS - 1:
+                return Z_COL
+            return S_COL
+
+        def e_col(n):
+            if 2 <= n <= UNITS - 3:
+                return G_COL
+            return 512
+
         def q_q(n, half):
             if half == 0:
                 qc = keep.tile([P, 512], U32, name="qc", align_bytes=64)
@@ -342,18 +364,21 @@ def tile_attention_pa_t_kernel(tc, query, context, query_bit, context_bit, W_in,
         t_x(3, 1)
         for i in range(UNITS):
             last = i == UNITS - 1
-            mask(i, 0)
             if i > 0:
                 m2(i, 2)
-                m2(i, 3)
                 recip(i - 1, 0, 4)
                 for k in range(4):
                     norm_g(i - 1, k)
                 store(i - 1, 0, 4)
             load(i + AHEAD)
-            mask(i, 1)
+            mask(i, 0)
+            if i > 0:
+                m2(i, 3)
             if i == 0:
                 q_x(2)
+            if 0 < i and i + 3 < UNITS and G_COL < 512:
+                regroup_g(i + 1, G_COL, 512)
+            mask(i, 1)
             if not last:
                 mask(i, 2)
                 mask(i, 3)
@@ -361,37 +386,46 @@ def tile_attention_pa_t_kernel(tc, query, context, query_bit, context_bit, W_in,
                 row_min(i, 2, 4)
             if i + 3 < UNITS:
                 c_x(i + 3, 0, scopy)
+            elif i + 2 < UNITS:
+                regroup(i + 1, T_COL, s_col(i + 1), scopy)
             if i + 2 < UNITS:
                 if i == 0:
                     m1(i + 2, 0)
                 drain(i + 2, 0)
+                m1(i + 2, 1)
             if i + 3 < UNITS:
                 c_x(i + 3, 1, scopy)
             if i + 2 < UNITS:
-                m1(i + 2, 1)
                 c_c(i + 2, scopy if i > 0 else vcopy)
             if i + 4 < UNITS:
                 t_x(i + 4, 0)
             if i + 2 < UNITS:
                 drain(i + 2, 1)
                 m1(i + 2, 2)
-                drain(i + 2, 2)
             if i + 4 < UNITS:
                 t_x(i + 4, 1)
+            if i + 3 < UNITS:
+                t_c(i + 3)
             if i + 2 < UNITS:
                 m1(i + 2, 3)
-            if i + 3 < UNITS:
-                idle_matmuls(IDLE)
-                t_c(i + 3)
             if not last:
+                idle_matmuls(IDLE)
                 for k in range(4):
                     exp(i, k)
                 if i + 2 < UNITS:
+                    drain(i + 2, 2)
                     drain(i + 2, 3)
-                    regroup(i + 2, S_COL, 512, scopy)
+                    if s_col(i + 2) < e_col(i + 2):
+                        regroup(i + 2, s_col(i + 2), e_col(i + 2), scopy)
                     q_c(i + 2)
-                regroup(i + 1, 0, 256, vcopy)
-                regroup(i + 1, 256, S_COL, vcopy)
+                if i + 3 < UNITS:
+                    regroup(i + 1, 0, 256, vcopy)
+                    if s_col(i + 1) > 256:
+                        regroup(i + 1, 256, s_col(i + 1), vcopy)
+                elif i + 2 < UNITS:
+                    regroup(i + 1, 0, T_COL, vcopy)
+                else:
+                    regroup(i + 1, 0, s_col(i + 1), vcopy)
                 if i % 2 == 1:
                     make_dead((i + 1) // 2)
                 q_q(i + 1, 0)

@@ -18,9 +18,8 @@ P = 128
 B, Q, K, D = 8, 1024, 512, 512
 FLOPS = 2 * (2 * B * Q * D * D)
 UNITS = 2 * B
-S_COL = 320
+S_COL = 384
 IDLE = 1
-G_COL = 384
 T_COL, Z_COL = 192, 128
 AHEAD = 6
 
@@ -186,25 +185,10 @@ def tile_attention_pa_t_kernel(tc, query, context, query_bit, context_bit, W_in,
                 in_=qb16[n][:, :, lo:hi].rearrange("p t (c i) -> p c t i", i=4),
             )
 
-        def regroup_g(n, lo, hi):
-            nc.gpsimd.tensor_scalar(
-                out=qg[n][:, lo:hi, :].rearrange("p (c i) t -> p c t i", i=4),
-                in0=qb16[n][:, :, lo:hi].rearrange("p t (c i) -> p c t i", i=4),
-                scalar1=1.0,
-                scalar2=0.0,
-                op0=ALU.mult,
-                op1=ALU.add,
-            )
-
         def s_col(n):
             if n == UNITS - 1:
                 return Z_COL
             return S_COL
-
-        def e_col(n):
-            if 2 <= n <= UNITS - 3:
-                return G_COL
-            return 512
 
         def q_q(n, half):
             if half == 0:
@@ -308,8 +292,8 @@ def tile_attention_pa_t_kernel(tc, query, context, query_bit, context_bit, W_in,
         bank_copy(scopy, Wg[:].bitcast(F32)[:, 0:2, :, :], ("w", 0))
         bank_copy(vcopy, Wg[:].bitcast(F32)[:, 2:4, :, :], ("w", 1))
         t_x(0, 0)
-        idle_matmuls(2)
         t_x(0, 1)
+        idle_matmuls(2)
         nc.vector.quantize_mx(
             out=Wc[:].bitcast(FP8X4), scales=Ws[:], in_=Wg[:].rearrange("p t m v -> p (t m v)")
         )
@@ -321,7 +305,6 @@ def tile_attention_pa_t_kernel(tc, query, context, query_bit, context_bit, W_in,
         q_x(0)
         c_c(0, vcopy)
         c_c(1, scopy)
-        idle_matmuls(2)
         for t in range(4):
             m1(0, t, in_score_bank=(t >= 2))
         drain(0, 0)
@@ -376,8 +359,6 @@ def tile_attention_pa_t_kernel(tc, query, context, query_bit, context_bit, W_in,
                 m2(i, 3)
             if i == 0:
                 q_x(2)
-            if 0 < i and i + 3 < UNITS and G_COL < 512:
-                regroup_g(i + 1, G_COL, 512)
             mask(i, 1)
             if not last:
                 mask(i, 2)
@@ -415,13 +396,11 @@ def tile_attention_pa_t_kernel(tc, query, context, query_bit, context_bit, W_in,
                 if i + 2 < UNITS:
                     drain(i + 2, 2)
                     drain(i + 2, 3)
-                    if s_col(i + 2) < e_col(i + 2):
-                        regroup(i + 2, s_col(i + 2), e_col(i + 2), scopy)
+                    regroup(i + 2, s_col(i + 2), 512, scopy)
                     q_c(i + 2)
                 if i + 3 < UNITS:
                     regroup(i + 1, 0, 256, vcopy)
-                    if s_col(i + 1) > 256:
-                        regroup(i + 1, 256, s_col(i + 1), vcopy)
+                    regroup(i + 1, 256, s_col(i + 1), vcopy)
                 elif i + 2 < UNITS:
                     regroup(i + 1, 0, T_COL, vcopy)
                 else:

@@ -20,7 +20,6 @@ FLOPS = 2 * (2 * B * Q * D * D)
 UNITS = 2 * B
 S_COL = 384
 IDLE = 1
-T_COL, Z_COL = 192, 128
 AHEAD = 6
 
 
@@ -50,9 +49,10 @@ def tile_attention_pa_t_kernel(tc, query, context, query_bit, context_bit, W_in,
         def load_x(n):
             b, h = n // 2, n % 2
             x_sb = xin.tile([P, 4, D], BF16, name="x_sb")
-            nc.sync.dma_start(
-                out=x_sb[:], in_=query[b].rearrange("(p t) k -> p t k", t=8)[:, 4 * h : 4 * h + 4, :]
-            )
+            rows = query[b].rearrange("(p t) k -> p t k", t=8)[:, 4 * h : 4 * h + 4, :]
+            step = 2 if n == 0 else 4
+            for r in range(0, 4, step):
+                nc.sync.dma_start(out=x_sb[:, r : r + step, :], in_=rows[:, r : r + step, :])
             x_raw[n] = x_sb
 
         def load_c(b):
@@ -74,7 +74,10 @@ def tile_attention_pa_t_kernel(tc, query, context, query_bit, context_bit, W_in,
                 load_cb(n // 2)
 
         W_sb = const.tile([P, 4, D], BF16, name="W_sb")
-        nc.sync.dma_start(out=W_sb[:], in_=W_in.rearrange("(m t) k -> m t k", t=4))
+        for r in range(0, 4, 2):
+            nc.sync.dma_start(
+                out=W_sb[:, r : r + 2, :], in_=W_in.rearrange("(m t) k -> m t k", t=4)[:, r : r + 2, :]
+            )
         b_bf = const.tile([P, 4], BF16, name="b_bf")
         qb_bf = const.tile([P, B, 8], BF16, name="qb_bf")
         with nc.allow_non_contiguous_dma(reason="two small vectors, loaded once"):
@@ -83,6 +86,7 @@ def tile_attention_pa_t_kernel(tc, query, context, query_bit, context_bit, W_in,
         for n in range(AHEAD):
             load(n)
 
+        gate = const.tile([P, 1], F32, name="gate")
         warm = const.tile([P, 1], F32, name="warm")
         nc.vector.memset(warm[:], 0.0)
         nc.scalar.activation(out=warm[:], in_=warm[:], func=ACT.Exp)
@@ -185,10 +189,17 @@ def tile_attention_pa_t_kernel(tc, query, context, query_bit, context_bit, W_in,
                 in_=qb16[n][:, :, lo:hi].rearrange("p t (c i) -> p c t i", i=4),
             )
 
-        def s_col(n):
-            if n == UNITS - 1:
-                return Z_COL
-            return S_COL
+        def regroup_g(n):
+            g = work.tile([P, 512, 4], BF16, name="qg", align_bytes=64)
+            qg[n] = g
+            nc.gpsimd.tensor_scalar(
+                out=g[:],
+                in0=qb16[n][:].rearrange("p t c -> p c t"),
+                scalar1=gate[:],
+                scalar2=0.0,
+                op0=ALU.mult,
+                op1=ALU.add,
+            )
 
         def q_q(n, half):
             if half == 0:
@@ -273,6 +284,11 @@ def tile_attention_pa_t_kernel(tc, query, context, query_bit, context_bit, W_in,
                 out=zs[n][:, k, :], in0=zs[n][:, k, :], scalar1=recs[n][:, k : k + 1], scalar2=None, op0=ALU.mult
             )
 
+        def norm_s(n, k):
+            nc.scalar.activation(
+                out=zs[n][:, k, :], in_=zs[n][:, k, :], func=ACT.Copy, scale=recs[n][:, k : k + 1]
+            )
+
         def store(n, lo, hi):
             b, h = n // 2, n % 2
             rows = out[b].rearrange("(p t) j -> p t j", t=8)
@@ -286,7 +302,7 @@ def tile_attention_pa_t_kernel(tc, query, context, query_bit, context_bit, W_in,
         Wg = const.tile([P, 4, P, 4], BF16, name="Wg", align_bytes=64)
         Wc = const.tile([P, 4 * P], U32, name="Wc", align_bytes=64)
         Ws = const.tile([P, 4 * P], U8, name="Ws", align_bytes=64)
-        idle_matmuls(7)
+        idle_matmuls(3)
         transposes(W_sb[:].bitcast(F32), 0, ("w", 0))
         transposes(W_sb[:].bitcast(F32), 2, ("w", 1))
         bank_copy(scopy, Wg[:].bitcast(F32)[:, 0:2, :, :], ("w", 0))
@@ -340,7 +356,7 @@ def tile_attention_pa_t_kernel(tc, query, context, query_bit, context_bit, W_in,
             drain(1, t)
             if t < 2:
                 m1(1, t + 2)
-        regroup(1, S_COL, 512, scopy)
+        regroup(1, 384, 512, scopy)
         t_x(3, 0)
         t_c(2)
         idle_matmuls(2)
@@ -349,62 +365,63 @@ def tile_attention_pa_t_kernel(tc, query, context, query_bit, context_bit, W_in,
             last = i == UNITS - 1
             if i > 0:
                 m2(i, 2)
-                recip(i - 1, 0, 4)
-                for k in range(4):
-                    norm_g(i - 1, k)
-                store(i - 1, 0, 4)
+            if 0 < i and not last:
+                nc.vector.memset(gate[:], 1.0)
+                regroup_g(i + 1)
             load(i + AHEAD)
             mask(i, 0)
             if i > 0:
                 m2(i, 3)
-            if i == 0:
-                q_x(2)
             mask(i, 1)
             if not last:
                 mask(i, 2)
+                if i > 0:
+                    recip(i - 1, 0, 4)
+                    norm_g(i - 1, 0)
                 mask(i, 3)
+                if i == 0:
+                    q_x(2)
                 row_min(i, 0, 2)
                 row_min(i, 2, 4)
             if i + 3 < UNITS:
                 c_x(i + 3, 0, scopy)
-            elif i + 2 < UNITS:
-                regroup(i + 1, T_COL, s_col(i + 1), scopy)
             if i + 2 < UNITS:
                 if i == 0:
                     m1(i + 2, 0)
+                    m1(i + 2, 1)
                 drain(i + 2, 0)
-                m1(i + 2, 1)
-            if i + 3 < UNITS:
-                c_x(i + 3, 1, scopy)
-            if i + 2 < UNITS:
-                c_c(i + 2, scopy if i > 0 else vcopy)
             if i + 4 < UNITS:
                 t_x(i + 4, 0)
             if i + 2 < UNITS:
-                drain(i + 2, 1)
                 m1(i + 2, 2)
+            if i + 3 < UNITS:
+                c_x(i + 3, 1, scopy)
             if i + 4 < UNITS:
                 t_x(i + 4, 1)
+            if i + 2 < UNITS:
+                drain(i + 2, 1)
+                m1(i + 2, 3)
+                idle_matmuls(IDLE)
+                drain(i + 2, 2)
+                c_c(i + 2, scopy if i > 0 else vcopy)
+                drain(i + 2, 3)
             if i + 3 < UNITS:
                 t_c(i + 3)
-            if i + 2 < UNITS:
-                m1(i + 2, 3)
-            if not last:
                 idle_matmuls(IDLE)
+            if not last:
+                if i > 0:
+                    norm_s(i - 1, 3)
                 for k in range(4):
                     exp(i, k)
+                if i > 0:
+                    norm_v(i - 1, 1)
                 if i + 2 < UNITS:
-                    drain(i + 2, 2)
-                    drain(i + 2, 3)
-                    regroup(i + 2, s_col(i + 2), 512, scopy)
                     q_c(i + 2)
-                if i + 3 < UNITS:
-                    regroup(i + 1, 0, 256, vcopy)
-                    regroup(i + 1, 256, s_col(i + 1), vcopy)
-                elif i + 2 < UNITS:
-                    regroup(i + 1, 0, T_COL, vcopy)
+                if i > 0:
+                    norm_v(i - 1, 2)
+                    store(i - 1, 0, 4)
                 else:
-                    regroup(i + 1, 0, s_col(i + 1), vcopy)
+                    regroup(1, 0, 384, vcopy)
                 if i % 2 == 1:
                     make_dead((i + 1) // 2)
                 q_q(i + 1, 0)
@@ -415,20 +432,31 @@ def tile_attention_pa_t_kernel(tc, query, context, query_bit, context_bit, W_in,
                 m2(i + 1, 1)
                 if i + 3 < UNITS:
                     m1(i + 3, 0)
+                    m1(i + 3, 1)
             else:
                 row_min(i, 0, 1)
+                recip(i - 1, 0, 4)
+                for k in range(2):
+                    norm_s(i - 1, 2 + k)
+                    norm_g(i - 1, k)
+                store(i - 1, 2, 4)
+                store(i - 1, 0, 2)
                 mask(i, 2)
                 row_min(i, 1, 2)
                 mask(i, 3)
                 row_min(i, 2, 3)
-                row_min(i, 3, 4)
-                for k in range(4):
+                for k in range(2):
                     exp(i, k)
                 recip(i, 0, 2)
+                row_min(i, 3, 4)
+                for k in range(2, 4):
+                    exp(i, k)
                 norm_v(i, 0)
                 norm_v(i, 1)
                 store(i, 0, 2)
-                for k in range(2, 4):
-                    recip(i, k, k + 1)
-                    norm_v(i, k)
-                    store(i, k, k + 1)
+                recip(i, 2, 3)
+                recip(i, 3, 4)
+                norm_v(i, 2)
+                store(i, 2, 3)
+                norm_v(i, 3)
+                store(i, 3, 4)

@@ -18,7 +18,7 @@ P = 128
 B, Q, K, D = 8, 1024, 512, 512
 FLOPS = 2 * (2 * B * Q * D * D)
 UNITS = 2 * B
-S_COL = 384
+G_COL = 256
 IDLE = 1
 AHEAD = 6
 
@@ -32,6 +32,7 @@ def tile_attention_pa_t_kernel(tc, query, context, query_bit, context_bit, W_in,
         work = ctx.enter_context(tc.tile_pool(name="work", bufs=3))
         keep = ctx.enter_context(tc.tile_pool(name="keep", bufs=4))
         soft = ctx.enter_context(tc.tile_pool(name="soft", bufs=4))
+        turn = ctx.enter_context(tc.tile_pool(name="turn", bufs=1))
         ps_t = ctx.enter_context(tc.psum_pool(name="ps_t", bufs=3))
         ps_q = ctx.enter_context(tc.psum_pool(name="ps_q", bufs=2))
         ps_s = ctx.enter_context(tc.psum_pool(name="ps_s", bufs=3))
@@ -86,7 +87,6 @@ def tile_attention_pa_t_kernel(tc, query, context, query_bit, context_bit, W_in,
         for n in range(AHEAD):
             load(n)
 
-        gate = const.tile([P, 1], F32, name="gate")
         warm = const.tile([P, 1], F32, name="warm")
         nc.vector.memset(warm[:], 0.0)
         nc.scalar.activation(out=warm[:], in_=warm[:], func=ACT.Exp)
@@ -182,7 +182,7 @@ def tile_attention_pa_t_kernel(tc, query, context, query_bit, context_bit, W_in,
 
         def regroup(n, lo, hi, copy):
             if n not in qg:
-                g = work.tile([P, 512, 4], BF16, name="qg", align_bytes=64)
+                g = turn.tile([P, 512, 4], BF16, name="qr", align_bytes=64)
                 qg[n] = g
             copy(
                 out=qg[n][:, lo:hi, :].rearrange("p (c i) t -> p c t i", i=4),
@@ -190,12 +190,12 @@ def tile_attention_pa_t_kernel(tc, query, context, query_bit, context_bit, W_in,
             )
 
         def regroup_g(n):
-            g = work.tile([P, 512, 4], BF16, name="qg", align_bytes=64)
+            g = turn.tile([P, 512, 4], BF16, name="qr", align_bytes=64)
             qg[n] = g
             nc.gpsimd.tensor_scalar(
                 out=g[:],
                 in0=qb16[n][:].rearrange("p t c -> p c t"),
-                scalar1=gate[:],
+                scalar1=1.0,
                 scalar2=0.0,
                 op0=ALU.mult,
                 op1=ALU.add,
@@ -269,19 +269,26 @@ def tile_attention_pa_t_kernel(tc, query, context, query_bit, context_bit, W_in,
         def recip(n, lo, hi):
             nc.vector.reciprocal(out=recs[n][:, lo:hi], in_=sums[n][:, lo:hi])
 
-        def norm_g(n, k):
+        def s_tile(n):
+            return 2 if n == UNITS - 4 else 3
+
+        def norm_g(n, k, hi=K):
             nc.gpsimd.tensor_scalar(
-                out=zs[n][:, k, :],
-                in0=zs[n][:, k, :],
+                out=zs[n][:, k, 0:hi],
+                in0=zs[n][:, k, 0:hi],
                 scalar1=recs[n][:, k : k + 1],
                 scalar2=0.0,
                 op0=ALU.mult,
                 op1=ALU.add,
             )
 
-        def norm_v(n, k):
+        def norm_v(n, k, lo=0):
             nc.vector.tensor_scalar(
-                out=zs[n][:, k, :], in0=zs[n][:, k, :], scalar1=recs[n][:, k : k + 1], scalar2=None, op0=ALU.mult
+                out=zs[n][:, k, lo:K],
+                in0=zs[n][:, k, lo:K],
+                scalar1=recs[n][:, k : k + 1],
+                scalar2=None,
+                op0=ALU.mult,
             )
 
         def norm_s(n, k):
@@ -302,7 +309,7 @@ def tile_attention_pa_t_kernel(tc, query, context, query_bit, context_bit, W_in,
         Wg = const.tile([P, 4, P, 4], BF16, name="Wg", align_bytes=64)
         Wc = const.tile([P, 4 * P], U32, name="Wc", align_bytes=64)
         Ws = const.tile([P, 4 * P], U8, name="Ws", align_bytes=64)
-        idle_matmuls(3)
+        idle_matmuls(4)
         transposes(W_sb[:].bitcast(F32), 0, ("w", 0))
         transposes(W_sb[:].bitcast(F32), 2, ("w", 1))
         bank_copy(scopy, Wg[:].bitcast(F32)[:, 0:2, :, :], ("w", 0))
@@ -316,79 +323,95 @@ def tile_attention_pa_t_kernel(tc, query, context, query_bit, context_bit, W_in,
         c_x(0, 0, scopy)
         c_x(0, 1, scopy)
         t_c(0)
-        t_c(1)
+        c_c(0, scopy)
         nc.vector.tensor_copy(out=b_f[:], in_=b_bf[:])
         q_x(0)
-        c_c(0, vcopy)
-        c_c(1, scopy)
-        for t in range(4):
-            m1(0, t, in_score_bank=(t >= 2))
+        m1(0, 0)
+        m1(0, 1)
+        m1(0, 2, in_score_bank=True)
+        m1(0, 3, in_score_bank=True)
+        t_c(1)
         drain(0, 0)
-        q_c(0)
         drain(0, 1, on_vector=True)
-        q_c(1)
         drain(0, 2)
         drain(0, 3, on_vector=True)
+        c_c(1, scopy)
         t_x(1, 0)
         t_x(1, 1)
+        q_c(0)
+        q_c(1)
         c_x(1, 0, scopy)
         make_dead(0)
         regroup(0, 0, 256, vcopy)
         regroup(0, 320, 512, scopy)
         regroup(0, 256, 320, vcopy)
+        idle_matmuls(2)
+        t_x(2, 0)
         q_q(0, 0)
         nc.vector.tensor_scalar(
             out=pa[:], in0=qb_bf[:].rearrange("p b t -> p (b t)"), scalar1=10000.0, scalar2=None, op0=ALU.mult
         )
         c_x(1, 1, scopy)
-        q_q(0, 1)
-        t_x(2, 0)
+        m2(0, 0)
+        m2(0, 1)
         t_x(2, 1)
-        for k in range(3):
-            m2(0, k)
+        q_q(0, 1)
         q_x(1)
         c_x(2, 0, scopy)
         c_x(2, 1, scopy)
         m1(1, 0)
+        m2(0, 2)
         m1(1, 1)
         m2(0, 3)
-        for t in range(4):
-            drain(1, t)
-            if t < 2:
-                m1(1, t + 2)
-        regroup(1, 384, 512, scopy)
+        drain(1, 0)
+        m1(1, 2)
+        drain(1, 1)
+        m1(1, 3)
+        drain(1, 2)
+        drain(1, 3)
         t_x(3, 0)
-        t_c(2)
-        idle_matmuls(2)
-        t_x(3, 1)
+        regroup(1, 384, 512, scopy)
         for i in range(UNITS):
             last = i == UNITS - 1
             if i > 0:
                 m2(i, 2)
             if 0 < i and not last:
-                nc.vector.memset(gate[:], 1.0)
                 regroup_g(i + 1)
             load(i + AHEAD)
             mask(i, 0)
             if i > 0:
                 m2(i, 3)
+                if i + 2 < UNITS:
+                    m1(i + 2, 1)
+                if i == 1:
+                    t_c(3)
+                    idle_matmuls(IDLE)
             mask(i, 1)
             if not last:
                 mask(i, 2)
                 if i > 0:
-                    recip(i - 1, 0, 4)
-                    norm_g(i - 1, 0)
+                    if i < UNITS - 2:
+                        recip(i - 1, 0, 4)
+                        norm_g(i - 1, 0, G_COL)
+                    else:
+                        recip(i - 1, 0, 2)
                 mask(i, 3)
                 if i == 0:
                     q_x(2)
                 row_min(i, 0, 2)
+                if i == UNITS - 2:
+                    q_q(i + 1, 0)
+                    m2(i + 1, 0)
+                    m2(i + 1, 1)
                 row_min(i, 2, 4)
             if i + 3 < UNITS:
                 c_x(i + 3, 0, scopy)
             if i + 2 < UNITS:
                 if i == 0:
-                    m1(i + 2, 0)
-                    m1(i + 2, 1)
+                    m1(2, 0)
+                    m1(2, 1)
+                    t_c(2)
+                    t_x(3, 1)
                 drain(i + 2, 0)
             if i + 4 < UNITS:
                 t_x(i + 4, 0)
@@ -405,58 +428,75 @@ def tile_attention_pa_t_kernel(tc, query, context, query_bit, context_bit, W_in,
                 drain(i + 2, 2)
                 c_c(i + 2, scopy if i > 0 else vcopy)
                 drain(i + 2, 3)
-            if i + 3 < UNITS:
+            if 0 < i < UNITS - 3:
                 t_c(i + 3)
-                idle_matmuls(IDLE)
+                idle_matmuls(2)
             if not last:
-                if i > 0:
-                    norm_s(i - 1, 3)
-                for k in range(4):
-                    exp(i, k)
-                if i > 0:
-                    norm_v(i - 1, 1)
-                if i + 2 < UNITS:
-                    q_c(i + 2)
-                if i > 0:
-                    norm_v(i - 1, 2)
-                    store(i - 1, 0, 4)
-                else:
+                if i == UNITS - 3:
+                    for k in range(4):
+                        exp(i, k)
+                if i == UNITS - 2:
+                    norm_s(i - 1, 0)
+                    norm_s(i - 1, 1)
+                    store(i - 1, 0, 2)
+                elif i > 0:
+                    for k in range(s_tile(i - 1), 4):
+                        norm_s(i - 1, k)
+                if i != UNITS - 3:
+                    for k in range(4):
+                        exp(i, k)
+                if i == 0:
+                    q_c(2)
                     regroup(1, 0, 384, vcopy)
+                elif i < UNITS - 2:
+                    norm_v(i - 1, 1)
+                    q_q(i + 1, 0)
+                    q_c(i + 2)
+                    if s_tile(i - 1) == 3:
+                        norm_v(i - 1, 2)
+                    norm_v(i - 1, 0, G_COL)
+                    store(i - 1, 0, 4)
                 if i % 2 == 1:
                     make_dead((i + 1) // 2)
-                q_q(i + 1, 0)
+                if i == 0:
+                    q_q(i + 1, 0)
                 if i + 3 < UNITS:
                     q_x(i + 3)
                 q_q(i + 1, 1)
-                m2(i + 1, 0)
-                m2(i + 1, 1)
+                if i == UNITS - 2:
+                    recip(i - 1, 2, 4)
+                else:
+                    m2(i + 1, 0)
+                    m2(i + 1, 1)
                 if i + 3 < UNITS:
                     m1(i + 3, 0)
-                    m1(i + 3, 1)
             else:
-                row_min(i, 0, 1)
+                norm_g(i - 2, 2)
+                norm_g(i - 2, 3)
+                store(i - 2, 2, 4)
                 recip(i - 1, 0, 4)
-                for k in range(2):
-                    norm_s(i - 1, 2 + k)
+                norm_s(i - 1, 0)
+                for k in range(2, 4):
                     norm_g(i - 1, k)
                 store(i - 1, 2, 4)
+                row_min(i, 0, 1)
+                exp(i, 0)
+                norm_s(i - 1, 1)
                 store(i - 1, 0, 2)
                 mask(i, 2)
                 row_min(i, 1, 2)
+                exp(i, 1)
+                recip(i, 0, 1)
+                norm_g(i, 0)
                 mask(i, 3)
                 row_min(i, 2, 3)
-                for k in range(2):
-                    exp(i, k)
-                recip(i, 0, 2)
+                exp(i, 2)
+                recip(i, 1, 2)
+                norm_g(i, 1)
                 row_min(i, 3, 4)
-                for k in range(2, 4):
-                    exp(i, k)
-                norm_v(i, 0)
-                norm_v(i, 1)
+                exp(i, 3)
                 store(i, 0, 2)
-                recip(i, 2, 3)
-                recip(i, 3, 4)
-                norm_v(i, 2)
-                store(i, 2, 3)
-                norm_v(i, 3)
-                store(i, 3, 4)
+                for k in range(2, 4):
+                    recip(i, k, k + 1)
+                    norm_v(i, k)
+                    store(i, k, k + 1)

@@ -40,7 +40,7 @@ def tile_attention_pa_t_kernel(tc, query, context, query_bit, context_bit, W_in,
         make_identity(nc, ident[:])
         ctx.enter_context(tc.manual_schedule())
 
-        x_raw, c_raw, cb_raw = {}, {}, {}
+        x_raw, c_raw = {}, {}
         banks = {}
         xg, xq, qb16, qg, qq = {}, {}, {}, {}, {}
         cg, cq = {}, {}
@@ -61,19 +61,15 @@ def tile_attention_pa_t_kernel(tc, query, context, query_bit, context_bit, W_in,
             nc.sync.dma_start(out=c_sb[:], in_=context[b].rearrange("(t p) k -> p t k", p=P))
             c_raw[b] = c_sb
 
-        def load_cb(b):
-            cb = cin.tile([P, K], BF16, name="cb")
-            nc.sync.dma_start(out=cb[:], in_=context_bit[b].partition_broadcast(P))
-            cb_raw[b] = cb
-
         def load(n):
             if n >= UNITS:
                 return
             load_x(n)
             if n % 2 == 0:
                 load_c(n // 2)
-                load_cb(n // 2)
 
+        warm = const.tile([P, 1], F32, name="warm")
+        nc.vector.memset(warm[:], 0.0)
         W_sb = const.tile([P, 4, D], BF16, name="W_sb")
         for r in range(0, 4, 2):
             nc.sync.dma_start(
@@ -83,16 +79,39 @@ def tile_attention_pa_t_kernel(tc, query, context, query_bit, context_bit, W_in,
         qb_bf = const.tile([P, B, 8], BF16, name="qb_bf")
         with nc.allow_non_contiguous_dma(reason="two small vectors, loaded once"):
             nc.scalar.dma_start(out=b_bf[:], in_=b_in.rearrange("(m t) -> m t", t=4))
-            nc.scalar.dma_start(out=qb_bf[:], in_=query_bit.rearrange("b (p t) -> p b t", t=8))
-        for n in range(AHEAD):
-            load(n)
+        bits = const.tile([P, (B - 1) * K], BF16, name="bits")
+        load(0)
+        load(1)
+        load_x(2)
+        brow = const.tile([P, K], BF16, name="brow")
+        nc.gpsimd.memset(brow[:], 0.0)
+        nc.sync.dma_start(out=brow[0:1, :], in_=context_bit[0:1, :])
+        with nc.allow_non_contiguous_dma(reason="a small vector, loaded once"):
+            nc.sync.dma_start(out=qb_bf[:], in_=query_bit.rearrange("b (p t) -> p b t", t=8))
+        load_c(1)
+        load_x(3)
+        load_x(4)
+        nc.sync.dma_start(out=bits[:], in_=context_bit[1:B].rearrange("b k -> (b k)").partition_broadcast(P))
+        load_c(2)
+        load_x(5)
 
-        warm = const.tile([P, 1], F32, name="warm")
-        nc.vector.memset(warm[:], 0.0)
         nc.scalar.activation(out=warm[:], in_=warm[:], func=ACT.Exp)
 
         zeros = const.tile([P, 512], BF16, name="zeros")
         nc.vector.memset(zeros[:], 0.0)
+
+        ones = const.tile([P, P], BF16, name="ones")
+        nc.vector.memset(ones[:], 1.0)
+
+        def spread_bits():
+            bp = ps_s.tile([P, K], F32, name="sp")
+            nc.tensor.matmul(bp[:], lhsT=ones[:], rhs=brow[:], start=True, stop=True)
+            banks["bits"] = bp
+
+        def first_dead():
+            d = keep.tile([P, K], BF16, name="dead")
+            nc.scalar.activation(out=d[:], in_=banks["bits"][:], func=ACT.Copy, scale=-1.0, bias=1.0)
+            dead[0] = d
 
         def idle_matmuls(count):
             idle = ps_s.tile([P, 512], F32, name="sp")
@@ -232,7 +251,7 @@ def tile_attention_pa_t_kernel(tc, query, context, query_bit, context_bit, W_in,
         def make_dead(b):
             d = keep.tile([P, K], BF16, name="dead")
             nc.vector.tensor_scalar(
-                out=d[:], in0=cb_raw[b][:], scalar1=-1.0, scalar2=1.0, op0=ALU.mult, op1=ALU.add
+                out=d[:], in0=bits[:, (b - 1) * K : b * K], scalar1=-1.0, scalar2=1.0, op0=ALU.mult, op1=ALU.add
             )
             dead[b] = d
 
@@ -341,17 +360,18 @@ def tile_attention_pa_t_kernel(tc, query, context, query_bit, context_bit, W_in,
         q_c(0)
         q_c(1)
         c_x(1, 0, scopy)
-        make_dead(0)
         regroup(0, 0, 256, vcopy)
         regroup(0, 320, 512, scopy)
         regroup(0, 256, 320, vcopy)
-        idle_matmuls(2)
+        spread_bits()
+        idle_matmuls(1)
         t_x(2, 0)
         q_q(0, 0)
         nc.vector.tensor_scalar(
             out=pa[:], in0=qb_bf[:].rearrange("p b t -> p (b t)"), scalar1=10000.0, scalar2=None, op0=ALU.mult
         )
         c_x(1, 1, scopy)
+        first_dead()
         m2(0, 0)
         m2(0, 1)
         t_x(2, 1)
@@ -382,20 +402,20 @@ def tile_attention_pa_t_kernel(tc, query, context, query_bit, context_bit, W_in,
             if i > 0:
                 m2(i, 3)
                 if i + 2 < UNITS:
-                    m1(i + 2, 1)
+                    m1(i + 2, 0)
                 if i == 1:
                     t_c(3)
                     idle_matmuls(IDLE)
             mask(i, 1)
             if not last:
                 mask(i, 2)
+                mask(i, 3)
                 if i > 0:
                     if i < UNITS - 2:
                         recip(i - 1, 0, 4)
                         norm_g(i - 1, 0, G_COL)
                     else:
                         recip(i - 1, 0, 2)
-                mask(i, 3)
                 if i == 0:
                     q_x(2)
                 row_min(i, 0, 2)
@@ -404,8 +424,8 @@ def tile_attention_pa_t_kernel(tc, query, context, query_bit, context_bit, W_in,
                     m2(i + 1, 0)
                     m2(i + 1, 1)
                 row_min(i, 2, 4)
-            if i + 3 < UNITS:
-                c_x(i + 3, 0, scopy)
+            if i == 0:
+                c_x(3, 0, scopy)
             if i + 2 < UNITS:
                 if i == 0:
                     m1(2, 0)
@@ -416,6 +436,8 @@ def tile_attention_pa_t_kernel(tc, query, context, query_bit, context_bit, W_in,
             if i + 4 < UNITS:
                 t_x(i + 4, 0)
             if i + 2 < UNITS:
+                if i > 0:
+                    m1(i + 2, 1)
                 m1(i + 2, 2)
             if i + 3 < UNITS:
                 c_x(i + 3, 1, scopy)
@@ -444,6 +466,8 @@ def tile_attention_pa_t_kernel(tc, query, context, query_bit, context_bit, W_in,
                         norm_s(i - 1, k)
                 if i != UNITS - 3:
                     for k in range(4):
+                        if k == 3 and i + 4 < UNITS:
+                            c_x(i + 4, 0, scopy)
                         exp(i, k)
                 if i == 0:
                     q_c(2)
@@ -468,8 +492,6 @@ def tile_attention_pa_t_kernel(tc, query, context, query_bit, context_bit, W_in,
                 else:
                     m2(i + 1, 0)
                     m2(i + 1, 1)
-                if i + 3 < UNITS:
-                    m1(i + 3, 0)
             else:
                 norm_g(i - 2, 2)
                 norm_g(i - 2, 3)

@@ -18,7 +18,7 @@ P = 128
 B, Q, K, D = 8, 1024, 512, 512
 FLOPS = 2 * (2 * B * Q * D * D)
 UNITS = 2 * B
-G_COL = 256
+G_COL = 512
 IDLE = 1
 AHEAD = 6
 
@@ -478,7 +478,6 @@ def tile_attention_pa_t_kernel(tc, query, context, query_bit, context_bit, W_in,
                     q_c(i + 2)
                     if s_tile(i - 1) == 3:
                         norm_v(i - 1, 2)
-                    norm_v(i - 1, 0, G_COL)
                     store(i - 1, 0, 4)
                 if i % 2 == 1:
                     make_dead((i + 1) // 2)

from contextlib import ExitStack

import concourse.bass as bass
import concourse.mybir as mybir
import concourse.tile as tile
from concourse.masks import make_identity

F32 = mybir.dt.float32
BF16 = mybir.dt.bfloat16
U32 = mybir.dt.uint32
U8 = mybir.dt.uint8
FP8X4 = mybir.dt.float8_e4m3fn_x4
ALU = mybir.AluOpType
ACT = mybir.ActivationFunctionType
AX = mybir.AxisListType

P = 128
B, Q, K, D = 8, 1024, 512, 512
FLOPS = 2 * (2 * B * Q * D * D)
UNITS = 2 * B
G_COL = 512
IDLE = 1
AHEAD = 6


def tile_attention_pa_t_kernel(tc, query, context, query_bit, context_bit, W_in, b_in, out):
    nc = tc.nc
    with ExitStack() as ctx:
        const = ctx.enter_context(tc.tile_pool(name="const", bufs=1))
        xin = ctx.enter_context(tc.tile_pool(name="xin", bufs=AHEAD + 1))
        cin = ctx.enter_context(tc.tile_pool(name="cin", bufs=4))
        work = ctx.enter_context(tc.tile_pool(name="work", bufs=3))
        keep = ctx.enter_context(tc.tile_pool(name="keep", bufs=4))
        soft = ctx.enter_context(tc.tile_pool(name="soft", bufs=4))
        turn = ctx.enter_context(tc.tile_pool(name="turn", bufs=1))
        ps_t = ctx.enter_context(tc.psum_pool(name="ps_t", bufs=3))
        ps_q = ctx.enter_context(tc.psum_pool(name="ps_q", bufs=2))
        ps_s = ctx.enter_context(tc.psum_pool(name="ps_s", bufs=3))
        ident = const.tile([P, P], F32, name="ident")
        make_identity(nc, ident[:])
        ctx.enter_context(tc.manual_schedule())

        x_raw, c_raw = {}, {}
        banks = {}
        xg, xq, qb16, qg, qq = {}, {}, {}, {}, {}
        cg, cq = {}, {}
        dead = {}
        zs, sums, mins, recs = {}, {}, {}, {}

        def load_x(n):
            b, h = n // 2, n % 2
            x_sb = xin.tile([P, 4, D], BF16, name="x_sb")
            rows = query[b].rearrange("(p t) k -> p t k", t=8)[:, 4 * h : 4 * h + 4, :]
            step = 2 if n == 0 else 4
            for r in range(0, 4, step):
                nc.sync.dma_start(out=x_sb[:, r : r + step, :], in_=rows[:, r : r + step, :])
            x_raw[n] = x_sb

        def load_c(b):
            c_sb = cin.tile([P, 4, D], BF16, name="c_sb")
            nc.sync.dma_start(out=c_sb[:], in_=context[b].rearrange("(t p) k -> p t k", p=P))
            c_raw[b] = c_sb

        def load(n):
            if n >= UNITS:
                return
            load_x(n)
            if n % 2 == 0:
                load_c(n // 2)

        warm = const.tile([P, 1], F32, name="warm")
        nc.vector.memset(warm[:], 0.0)
        W_sb = const.tile([P, 4, D], BF16, name="W_sb")
        for r in range(0, 4, 2):
            nc.sync.dma_start(
                out=W_sb[:, r : r + 2, :], in_=W_in.rearrange("(m t) k -> m t k", t=4)[:, r : r + 2, :]
            )
        b_bf = const.tile([P, 4], BF16, name="b_bf")
        qb_bf = const.tile([P, B, 8], BF16, name="qb_bf")
        with nc.allow_non_contiguous_dma(reason="two small vectors, loaded once"):
            nc.scalar.dma_start(out=b_bf[:], in_=b_in.rearrange("(m t) -> m t", t=4))
        bits = const.tile([P, (B - 1) * K], BF16, name="bits")
        load(0)
        load(1)
        load_x(2)
        brow = const.tile([P, K], BF16, name="brow")
        nc.gpsimd.memset(brow[:], 0.0)
        nc.sync.dma_start(out=brow[0:1, :], in_=context_bit[0:1, :])
        with nc.allow_non_contiguous_dma(reason="a small vector, loaded once"):
            nc.sync.dma_start(out=qb_bf[:], in_=query_bit.rearrange("b (p t) -> p b t", t=8))
        load_c(1)
        load_x(3)
        load_x(4)
        nc.sync.dma_start(out=bits[:], in_=context_bit[1:B].rearrange("b k -> (b k)").partition_broadcast(P))
        load_c(2)
        load_x(5)

        nc.scalar.activation(out=warm[:], in_=warm[:], func=ACT.Exp)

        zeros = const.tile([P, 512], BF16, name="zeros")
        nc.vector.memset(zeros[:], 0.0)

        ones = const.tile([P, P], BF16, name="ones")
        nc.vector.memset(ones[:], 1.0)

        def spread_bits():
            bp = ps_s.tile([P, K], F32, name="sp")
            nc.tensor.matmul(bp[:], lhsT=ones[:], rhs=brow[:], start=True, stop=True)
            banks["bits"] = bp

        def first_dead():
            d = keep.tile([P, K], BF16, name="dead")
            nc.scalar.activation(out=d[:], in_=banks["bits"][:], func=ACT.Copy, scale=-1.0, bias=1.0)
            dead[0] = d

        def idle_matmuls(count):
            idle = ps_s.tile([P, 512], F32, name="sp")
            for j in range(count):
                nc.tensor.matmul(idle[:], lhsT=zeros[:, 0:P], rhs=zeros[:], start=True, stop=True)

        def transposes(src, row, key):
            tp = ps_t.tile([P, 4, P], F32, name="tp")
            for a in range(2):
                for u in range(2):
                    nc.tensor.transpose(tp[:, 2 * a + u, :], src[:, row + a, u : 2 * P : 2], ident[:])
            banks[key] = tp

        def bank_copy(copy, dst, key):
            tp = banks[key]
            copy(out=dst, in_=tp[:].rearrange("p (a u) m -> p a m u", a=2))

        def t_x(n, pair):
            transposes(x_raw[n][:].bitcast(F32), 2 * pair, ("x", n, pair))

        def c_x(n, pair, copy):
            if n not in xg:
                g = work.tile([P, 4, P, 4], BF16, name="g", align_bytes=64)
                xg[n] = g
            bank_copy(copy, xg[n][:].bitcast(F32)[:, 2 * pair : 2 * pair + 2, :, :], ("x", n, pair))

        def q_x(n):
            xc = keep.tile([P, 512], U32, name="xc", align_bytes=64)
            xs = keep.tile([P, 512], U8, name="xs", align_bytes=64)
            nc.vector.quantize_mx(
                out=xc[:].bitcast(FP8X4), scales=xs[:], in_=xg[n][:].rearrange("p t m v -> p (t m v)")
            )
            xq[n] = (xc, xs)

        def t_c(i):
            transposes(c_raw[i // 2][:].bitcast(F32), 2 * (i % 2), ("c", i))

        def c_c(i, copy):
            g = work.tile([P, 2, P, 4], BF16, name="cgrp", align_bytes=64)
            cg[i] = g
            bank_copy(copy, g[:].bitcast(F32), ("c", i))

        def q_c(i):
            b, half = i // 2, i % 2
            if half == 0:
                cc = keep.tile([P, K], U32, name="cc", align_bytes=64)
                cs = keep.tile([P, K], U8, name="cs", align_bytes=64)
                cq[b] = (cc, cs)
            cc, cs = cq[b]
            cols = slice(256 * half, 256 * half + 256)
            nc.vector.quantize_mx(
                out=cc[:, cols].bitcast(FP8X4),
                scales=cs[:, cols],
                in_=cg[i][:].rearrange("p t m v -> p (t m v)"),
            )

        def m1(n, t, in_score_bank=False):
            xc, xs = xq[n]
            if in_score_bank:
                qp = ps_s.tile([P, 512], F32, name="sp")
            else:
                qp = ps_q.tile([P, 512], F32, name="qp")
            nc.tensor.matmul_mx(
                out=qp[:],
                lhsT=Wc[:, P * t : P * (t + 1)].bitcast(FP8X4),
                lhsT_scale=Ws[:, P * t : P * (t + 1)],
                rhs=xc[:].bitcast(FP8X4),
                rhs_scale=xs[:],
                start=True,
                stop=True,
            )
            banks["q", n, t] = qp

        def drain(n, t, on_vector=False):
            if n not in qb16:
                q_bf = work.tile([P, 4, 512], BF16, name="q_bf")
                qb16[n] = q_bf
            qp = banks["q", n, t]
            if on_vector:
                nc.vector.tensor_scalar(
                    out=qb16[n][:, t, :], in0=qp[:], scalar1=b_f[:, t : t + 1], scalar2=None, op0=ALU.add
                )
            else:
                nc.scalar.activation(
                    out=qb16[n][:, t, :], in_=qp[:], func=ACT.Identity, bias=b_f[:, t : t + 1], scale=1.0
                )

        def regroup(n, lo, hi, copy):
            if n not in qg:
                g = turn.tile([P, 512, 4], BF16, name="qr", align_bytes=64)
                qg[n] = g
            copy(
                out=qg[n][:, lo:hi, :].rearrange("p (c i) t -> p c t i", i=4),
                in_=qb16[n][:, :, lo:hi].rearrange("p t (c i) -> p c t i", i=4),
            )

        def regroup_g(n):
            g = turn.tile([P, 512, 4], BF16, name="qr", align_bytes=64)
            qg[n] = g
            nc.gpsimd.tensor_scalar(
                out=g[:],
                in0=qb16[n][:].rearrange("p t c -> p c t"),
                scalar1=1.0,
                scalar2=0.0,
                op0=ALU.mult,
                op1=ALU.add,
            )

        def q_q(n, half):
            if half == 0:
                qc = keep.tile([P, 512], U32, name="qc", align_bytes=64)
                qs = keep.tile([P, 512], U8, name="qs", align_bytes=64)
                qq[n] = (qc, qs)
            qc, qs = qq[n]
            cols = slice(256 * half, 256 * half + 256)
            nc.vector.quantize_mx(
                out=qc[:, cols].bitcast(FP8X4),
                scales=qs[:, cols],
                in_=qg[n][:, cols, :].rearrange("p c t -> p (c t)"),
            )

        def m2(n, k):
            qc, qs = qq[n]
            cc, cs = cq[n // 2]
            sp = ps_s.tile([P, K], F32, name="sp")
            nc.tensor.matmul_mx(
                out=sp[:],
                lhsT=qc[:, P * k : P * (k + 1)].bitcast(FP8X4),
                lhsT_scale=qs[:, P * k : P * (k + 1)],
                rhs=cc[:].bitcast(FP8X4),
                rhs_scale=cs[:],
                start=True,
                stop=True,
            )
            banks["s", n, k] = sp

        def make_dead(b):
            d = keep.tile([P, K], BF16, name="dead")
            nc.vector.tensor_scalar(
                out=d[:], in0=bits[:, (b - 1) * K : b * K], scalar1=-1.0, scalar2=1.0, op0=ALU.mult, op1=ALU.add
            )
            dead[b] = d

        def mask(n, k):
            if k == 0:
                z = soft.tile([P, 4, K], F32, name="z")
                nm = soft.tile([P, 4], F32, name="nm")
                ssum = soft.tile([P, 4], F32, name="ssum")
                r = soft.tile([P, 4], F32, name="r")
                zs[n], mins[n], sums[n], recs[n] = z, nm, ssum, r
            col = 4 * n + k
            nc.vector.scalar_tensor_tensor(
                out=zs[n][:, k, :],
                in0=dead[n // 2][:],
                scalar=pa[:, col : col + 1],
                in1=banks["s", n, k][:],
                op0=ALU.mult,
                op1=ALU.subtract,
            )

        def row_min(n, lo, hi):
            nc.vector.tensor_reduce(out=mins[n][:, lo:hi], in_=zs[n][:, lo:hi, :], axis=AX.X, op=ALU.min)

        def exp(n, k):
            nc.scalar.activation(
                out=zs[n][:, k, :],
                in_=zs[n][:, k, :],
                func=ACT.Exp,
                bias=mins[n][:, k : k + 1],
                scale=-1.0,
                accum_out=sums[n][:, k : k + 1],
            )

        def recip(n, lo, hi):
            nc.vector.reciprocal(out=recs[n][:, lo:hi], in_=sums[n][:, lo:hi])

        def s_tile(n):
            return 2 if n == UNITS - 4 else 3

        def norm_g(n, k, hi=K):
            nc.gpsimd.tensor_scalar(
                out=zs[n][:, k, 0:hi],
                in0=zs[n][:, k, 0:hi],
                scalar1=recs[n][:, k : k + 1],
                scalar2=0.0,
                op0=ALU.mult,
                op1=ALU.add,
            )

        def norm_v(n, k, lo=0):
            nc.vector.tensor_scalar(
                out=zs[n][:, k, lo:K],
                in0=zs[n][:, k, lo:K],
                scalar1=recs[n][:, k : k + 1],
                scalar2=None,
                op0=ALU.mult,
            )

        def norm_s(n, k):
            nc.scalar.activation(
                out=zs[n][:, k, :], in_=zs[n][:, k, :], func=ACT.Copy, scale=recs[n][:, k : k + 1]
            )

        def store(n, lo, hi):
            b, h = n // 2, n % 2
            rows = out[b].rearrange("(p t) j -> p t j", t=8)
            nc.sync.dma_start(out=rows[:, 4 * h + lo : 4 * h + hi, :], in_=zs[n][:, lo:hi, :])

        vcopy = nc.vector.tensor_copy
        scopy = nc.scalar.copy

        b_f = const.tile([P, 4], F32, name="b_f")
        pa = const.tile([P, B * 8], F32, name="pa")
        Wg = const.tile([P, 4, P, 4], BF16, name="Wg", align_bytes=64)
        Wc = const.tile([P, 4 * P], U32, name="Wc", align_bytes=64)
        Ws = const.tile([P, 4 * P], U8, name="Ws", align_bytes=64)
        idle_matmuls(4)
        transposes(W_sb[:].bitcast(F32), 0, ("w", 0))
        transposes(W_sb[:].bitcast(F32), 2, ("w", 1))
        bank_copy(scopy, Wg[:].bitcast(F32)[:, 0:2, :, :], ("w", 0))
        bank_copy(vcopy, Wg[:].bitcast(F32)[:, 2:4, :, :], ("w", 1))
        t_x(0, 0)
        t_x(0, 1)
        idle_matmuls(2)
        nc.vector.quantize_mx(
            out=Wc[:].bitcast(FP8X4), scales=Ws[:], in_=Wg[:].rearrange("p t m v -> p (t m v)")
        )
        c_x(0, 0, scopy)
        c_x(0, 1, scopy)
        t_c(0)
        c_c(0, scopy)
        nc.vector.tensor_copy(out=b_f[:], in_=b_bf[:])
        q_x(0)
        m1(0, 0)
        m1(0, 1)
        m1(0, 2, in_score_bank=True)
        m1(0, 3, in_score_bank=True)
        t_c(1)
        drain(0, 0)
        drain(0, 1, on_vector=True)
        drain(0, 2)
        drain(0, 3, on_vector=True)
        c_c(1, scopy)
        t_x(1, 0)
        t_x(1, 1)
        q_c(0)
        q_c(1)
        c_x(1, 0, scopy)
        regroup(0, 0, 256, vcopy)
        regroup(0, 320, 512, scopy)
        regroup(0, 256, 320, vcopy)
        spread_bits()
        idle_matmuls(1)
        t_x(2, 0)
        q_q(0, 0)
        nc.vector.tensor_scalar(
            out=pa[:], in0=qb_bf[:].rearrange("p b t -> p (b t)"), scalar1=10000.0, scalar2=None, op0=ALU.mult
        )
        c_x(1, 1, scopy)
        first_dead()
        m2(0, 0)
        m2(0, 1)
        t_x(2, 1)
        q_q(0, 1)
        q_x(1)
        c_x(2, 0, scopy)
        c_x(2, 1, scopy)
        m1(1, 0)
        m2(0, 2)
        m1(1, 1)
        m2(0, 3)
        drain(1, 0)
        m1(1, 2)
        drain(1, 1)
        m1(1, 3)
        drain(1, 2)
        drain(1, 3)
        t_x(3, 0)
        regroup(1, 384, 512, scopy)
        for i in range(UNITS):
            last = i == UNITS - 1
            if i > 0:
                m2(i, 2)
            if 0 < i and not last:
                regroup_g(i + 1)
            load(i + AHEAD)
            mask(i, 0)
            if i > 0:
                m2(i, 3)
                if i + 2 < UNITS:
                    m1(i + 2, 0)
                if i == 1:
                    t_c(3)
                    idle_matmuls(IDLE)
            mask(i, 1)
            if not last:
                mask(i, 2)
                mask(i, 3)
                if i > 0:
                    if i < UNITS - 2:
                        recip(i - 1, 0, 4)
                        norm_g(i - 1, 0, G_COL)
                    else:
                        recip(i - 1, 0, 2)
                if i == 0:
                    q_x(2)
                row_min(i, 0, 2)
                if i == UNITS - 2:
                    q_q(i + 1, 0)
                    m2(i + 1, 0)
                    m2(i + 1, 1)
                row_min(i, 2, 4)
            if i == 0:
                c_x(3, 0, scopy)
            if i + 2 < UNITS:
                if i == 0:
                    m1(2, 0)
                    m1(2, 1)
                    t_c(2)
                    t_x(3, 1)
                drain(i + 2, 0)
            if i + 4 < UNITS:
                t_x(i + 4, 0)
            if i + 2 < UNITS:
                if i > 0:
                    m1(i + 2, 1)
                m1(i + 2, 2)
            if i + 3 < UNITS:
                c_x(i + 3, 1, scopy)
            if i + 4 < UNITS:
                t_x(i + 4, 1)
            if i + 2 < UNITS:
                drain(i + 2, 1)
                m1(i + 2, 3)
                idle_matmuls(IDLE)
                drain(i + 2, 2)
                c_c(i + 2, scopy if i > 0 else vcopy)
                drain(i + 2, 3)
            if 0 < i < UNITS - 3:
                t_c(i + 3)
                idle_matmuls(2)
            if not last:
                if i == UNITS - 3:
                    for k in range(4):
                        exp(i, k)
                if i == UNITS - 2:
                    norm_s(i - 1, 0)
                    norm_s(i - 1, 1)
                    store(i - 1, 0, 2)
                elif i > 0:
                    for k in range(s_tile(i - 1), 4):
                        norm_s(i - 1, k)
                if i != UNITS - 3:
                    for k in range(4):
                        if k == 3 and i + 4 < UNITS:
                            c_x(i + 4, 0, scopy)
                        exp(i, k)
                if i == 0:
                    q_c(2)
                    regroup(1, 0, 384, vcopy)
                elif i < UNITS - 2:
                    norm_v(i - 1, 1)
                    q_q(i + 1, 0)
                    q_c(i + 2)
                    if s_tile(i - 1) == 3:
                        norm_v(i - 1, 2)
                    store(i - 1, 0, 4)
                if i % 2 == 1:
                    make_dead((i + 1) // 2)
                if i == 0:
                    q_q(i + 1, 0)
                if i + 3 < UNITS:
                    q_x(i + 3)
                q_q(i + 1, 1)
                if i == UNITS - 2:
                    recip(i - 1, 2, 4)
                else:
                    m2(i + 1, 0)
                    m2(i + 1, 1)
            else:
                norm_g(i - 2, 2)
                norm_g(i - 2, 3)
                store(i - 2, 2, 4)
                recip(i - 1, 0, 4)
                norm_s(i - 1, 0)
                for k in range(2, 4):
                    norm_g(i - 1, k)
                store(i - 1, 2, 4)
                row_min(i, 0, 1)
                exp(i, 0)
                norm_s(i - 1, 1)
                store(i - 1, 0, 2)
                mask(i, 2)
                row_min(i, 1, 2)
                exp(i, 1)
                recip(i, 0, 1)
                norm_g(i, 0)
                mask(i, 3)
                row_min(i, 2, 3)
                exp(i, 2)
                recip(i, 1, 2)
                norm_g(i, 1)
                row_min(i, 3, 4)
                exp(i, 3)
                store(i, 0, 2)
                for k in range(2, 4):
                    recip(i, k, k + 1)
                    norm_v(i, k)
                    store(i, k, k + 1)
